import numpy as np
import ml_dtypes


def mxq(x, axis, fmt="e4m3"):
    dtype, down = {"e4m3": (ml_dtypes.float8_e4m3fn, 7), "e5m2": (ml_dtypes.float8_e5m2, 14)}[fmt]
    v = np.moveaxis(np.asarray(x, np.float32).astype(ml_dtypes.bfloat16).astype(np.float64), axis, -1)
    blocks = v.reshape(v.shape[:-1] + (-1, 32))
    amax = np.abs(blocks).max(-1, keepdims=True)
    byte = np.maximum(np.where(amax > 0, np.frexp(amax)[1] - 1 + 127, 0) - down, 1)
    scale = np.exp2(byte - 127.0)
    codes = (blocks / scale).astype(np.float32).astype(dtype).astype(np.float64)
    return np.moveaxis((codes * scale).reshape(v.shape), -1, axis)


WIDE = False


def mx_kscale(k):
    if not WIDE:
        return np.ones(k)
    levels = np.array([10, -10, 5, -5, 0])
    if k % 512:
        return np.exp2(np.random.permutation(np.resize(levels, k // 32))).repeat(32)
    a = np.empty((k // 512, 16))
    for p in range(k // 512):
        a[p, :8] = np.random.permutation(np.resize(levels, 8))
        for g in range(8):
            far = levels[np.abs(levels - a[p, g]) >= 10]
            a[p, g + 8] = far[np.random.randint(len(far))]
    return np.exp2(a.ravel()).repeat(32)


BF16 = ml_dtypes.bfloat16


def bf(x):
    return np.asarray(x, np.float32).astype(BF16)


def f64(x):
    return np.asarray(x).astype(np.float64)


B, A, E, P, R = 256, 8, 512, 512, 512


def setup_inputs():
    s_src, s_edge = mx_kscale(E), mx_kscale(E)
    t = mx_kscale(P)
    s_cat = np.concatenate([s_src, s_edge])
    return {
        "image_features": bf(np.random.standard_normal((B, E)) * s_src),
        "edge_attributes": bf(np.random.standard_normal((B, A, E)) * s_edge),
        "linear_w": bf(np.random.standard_normal((P, 2 * E)) / np.sqrt(2 * E) / s_cat * t[:, None]),
        "linear_b": bf(np.random.standard_normal(P) * 0.3 * t),
        "fwd_proj": bf(np.random.standard_normal((A, P, R)) / np.sqrt(P) / t[:, None]),
    }


def reference(image_features, edge_attributes, linear_w, linear_b, fwd_proj):
    w = f64(linear_w)
    node = mxq(f64(image_features), 1, "e4m3") @ mxq(w[:, :E].T, 0, "e4m3")
    edge = (mxq(f64(edge_attributes).reshape(B * A, E), 1, "e4m3") @ mxq(w[:, E:].T, 0, "e4m3")).reshape(B, A, P)
    agg = node[:, None, :] + edge + f64(linear_b)
    rep = mxq(agg.transpose(1, 0, 2), 2, "e4m3") @ mxq(f64(fwd_proj), 1, "e4m3")
    return rep.transpose(1, 0, 2)

@@ -1,0 +1,185 @@
+from contextlib import ExitStack
+
+import concourse.mybir as mybir
+from concourse.masks import make_identity
+
+F32 = mybir.dt.float32
+BF16 = mybir.dt.bfloat16
+U32 = mybir.dt.uint32
+U8 = mybir.dt.uint8
+FP8X4 = mybir.dt.float8_e4m3fn_x4
+ADD = mybir.AluOpType.add
+
+NB, NA, NE, NP, NR = 256, 8, 512, 512, 512
+FLOPS = 2 * (NB + NB * NA) * NE * NP + 2 * NB * NA * NP * NR
+P = 128
+BANK_DT = F32
+ON_VECTOR = ['oc_7_1']
+FI_V_COLS = [224,224,224,224,224,224,224,224]
+SPLIT_STORES = [7]
+ORDER = """LF_0 LW_0 LW_1 LW_2 LW_3 LI LE_0 LF_1 LF_2 LE_1 LF_3 LF_4 LE_2 LF_5 LF_6 LE_3 LF_7 fi_0_0 fi_0_1 wtr_0 wcp_0 wtr_1 wcp_1 wtr_2 wcp_2 wtr_3 wcp_3 qf_0 wq_0 wq_1 itr icp wq_2 wq_3 tr_0 cp_0 iq tr_1 cp_1 nd_0 nd_1 fi_1_0 fi_1_1 nb_0 nb_1 qe_0 s1_0_0 s1_0_1 tr_2 cp_2 ad_0_0 ad_0_1 qe_1 s1_1_0 s1_1_1 tr_3 cp_3 qa_0 fi_2_0 fi_2_1 qf_1 s2_0_0 s2_0_1 oc_0_0 oc_0_1 st_0 ad_1_0 ad_1_1 qe_2 s1_2_0 s1_2_1 tr_4 cp_4 qa_1 fi_3_0 fi_3_1 qf_2 s2_1_0 s2_1_1 oc_1_0 oc_1_1 st_1 ad_2_0 ad_2_1 qe_3 s1_3_0 s1_3_1 tr_5 cp_5 qa_2 fi_4_0 fi_4_1 qf_3 s2_2_0 s2_2_1 oc_2_0 oc_2_1 st_2 ad_3_0 ad_3_1 qe_4 s1_4_0 s1_4_1 tr_6 cp_6 qa_3 fi_5_0 fi_5_1 qf_4 s2_3_0 s2_3_1 oc_3_0 oc_3_1 st_3 ad_4_0 ad_4_1 qe_5 s1_5_0 s1_5_1 tr_7 cp_7 qa_4 fi_6_0 fi_6_1 qf_5 s2_4_0 s2_4_1 oc_4_0 oc_4_1 st_4 ad_5_0 ad_5_1 qe_6 s1_6_0 s1_6_1 qa_5 fi_7_0 fi_7_1 qf_6 s2_5_0 s2_5_1 oc_5_0 oc_5_1 st_5 ad_6_0 ad_6_1 qe_7 s1_7_0 s1_7_1 qa_6 qf_7 s2_6_0 s2_6_1 oc_6_0 oc_6_1 st_6 ad_7_0 ad_7_1 qa_7 s2_7_0 s2_7_1 oc_7_0 st_7_0 oc_7_1 st_7_1"""
+
+
+def tile_attributegnn_pa_kernel(tc, image_features, edge_attributes, linear_w, linear_b, fwd_proj, out):
+    nc = tc.nc
+    with ExitStack() as ctx:
+        sb = ctx.enter_context(tc.tile_pool(name="sb", bufs=1))
+        ps = ctx.enter_context(tc.psum_pool(name="ps", bufs=1))
+        ctx.enter_context(tc.manual_schedule())
+
+        ident = sb.tile([P, P], F32, name="ident", tag="ident")
+        make_identity(nc, ident[:])
+        bias_sb = sb.tile([P, 4], BF16, name="bias_sb", tag="bias_sb")
+        nc.scalar.dma_start(out=bias_sb[:], in_=linear_b.rearrange("(p t) -> p t", t=4))
+
+        w_view = linear_w.rearrange("(m t) k -> m t k", t=4)
+        edge_view = edge_attributes.rearrange("(g p) a k -> p g a k", p=P)
+        out_view = out.rearrange("(g p) a r -> p g a r", p=P)
+        T = {}
+
+        def copy_engine(tok):
+            return nc.vector.tensor_copy if tok in ON_VECTOR else nc.scalar.copy
+
+        def LW(tok, t):
+            T["w_raw", t] = sb.tile([P, 2 * NE], BF16, name="w_raw%d" % t, tag="w_raw%d" % t)
+            nc.sync.dma_start(out=T["w_raw", t][:], in_=w_view[:, t, :])
+
+        def LI(tok):
+            T["i_raw"] = sb.tile([P, 2, NE], BF16, name="i_raw", tag="i_raw")
+            nc.sync.dma_start(out=T["i_raw"][:], in_=image_features.rearrange("(g p) k -> p g k", p=P))
+
+        def LE(tok, i):
+            T["e_raw", i] = sb.tile([P, 2, 2, NE], BF16, name="e_raw%d" % i, tag="e_raw%d" % i)
+            nc.sync.dma_start(out=T["e_raw", i][:], in_=edge_view[:, :, 2 * i : 2 * i + 2, :])
+
+        def LF(tok, a):
+            T["f_raw", a] = sb.tile([P, 4, NR], BF16, name="f_raw%d" % a, tag="f_raw%d" % a)
+            nc.sync.dma_start(out=T["f_raw", a][:], in_=fwd_proj[a].rearrange("(p j) r -> p j r", j=4))
+
+        def transposes(srcs, name):
+            tp = ps.tile([P, 2, 2, P], F32, name=name, tag="tp", bufs=2)
+            for g in (0, 1):
+                words = srcs[g].bitcast(F32)
+                for u in (0, 1):
+                    nc.tensor.transpose(tp[:, g, u, :], words[:, u : NE // 2 : 2], ident[:])
+            return tp
+
+        def copy_out(tok, tp, name, tag, bufs):
+            grp = sb.tile([P, 2, P, 4], BF16, name=name, tag=tag, bufs=bufs, align_bytes=64)
+            copy_engine(tok)(out=grp[:].bitcast(F32), in_=tp[:].rearrange("p g u b -> p g b u"))
+            return grp
+
+        def quantize(grp_flat, width, name):
+            codes = sb.tile([P, width // 4], U32, name=name + "_c", tag=name + "_c", align_bytes=64)
+            scales = sb.tile([P, width // 4], U8, name=name + "_s", tag=name + "_s", align_bytes=64)
+            nc.vector.quantize_mx(out=codes[:].bitcast(FP8X4), scales=scales[:], in_=grp_flat)
+            return codes, scales
+
+        def mx(out_ap, lhs, lcols, rhs, rcols):
+            nc.tensor.matmul_mx(
+                out=out_ap,
+                lhsT=lhs[0][:, lcols].bitcast(FP8X4),
+                lhsT_scale=lhs[1][:, lcols],
+                rhs=rhs[0][:, rcols].bitcast(FP8X4),
+                rhs_scale=rhs[1][:, rcols],
+                start=True,
+                stop=True,
+            )
+
+        def stage1(x_q, g, h, name):
+            bank = ps.tile([P, 4, P], BANK_DT, name=name, tag="s1", bufs=3)
+            for t in range(4):
+                mx(bank[:, t, :], T["w_q", t], slice(h * P, (h + 1) * P), x_q, slice(g * P, (g + 1) * P))
+            return bank
+
+        def wtr(tok, t):
+            T["w_tp", t] = transposes([T["w_raw", t][:, 0:NE], T["w_raw", t][:, NE : 2 * NE]], "w_tp")
+
+        def wcp(tok, t):
+            T["w_grp", t] = copy_out(tok, T["w_tp", t], "w_grp%d" % t, "w_grp%d" % t, 1)
+
+        def wq(tok, t):
+            T["w_q", t] = quantize(T["w_grp", t][:].rearrange("p g b j -> p (g b j)"), 1024, "w_q%d" % t)
+
+        def itr(tok):
+            T["i_tp"] = transposes([T["i_raw"][:, 0, :], T["i_raw"][:, 1, :]], "i_tp")
+
+        def icp(tok):
+            T["i_grp"] = copy_out(tok, T["i_tp"], "i_grp", "i_grp", 1)
+
+        def iq(tok):
+            T["i_q"] = quantize(T["i_grp"][:].rearrange("p g b j -> p (g b j)"), 1024, "i_q")
+
+        def nd(tok, g):
+            T["n_bank", g] = stage1(T["i_q"], g, 0, "n_bank")
+
+        def nb(tok, g):
+            T["nodeb", g] = sb.tile([P, P, 4], F32, name="nodeb%d" % g, tag="nodeb%d" % g)
+            nc.vector.tensor_tensor(
+                out=T["nodeb", g][:],
+                in0=T["n_bank", g][:].rearrange("p t b -> p b t"),
+                in1=bias_sb[:].unsqueeze(1).to_broadcast([P, P, 4]),
+                op=ADD,
+            )
+
+        def tr(tok, a):
+            er = T["e_raw", a // 2]
+            T["e_tp", a] = transposes([er[:, 0, a % 2, :], er[:, 1, a % 2, :]], "e_tp")
+
+        def cp(tok, a):
+            T["e_grp", a] = copy_out(tok, T["e_tp", a], "e_grp", "e_grp", 4)
+
+        def qe(tok, a):
+            T["e_q", a] = quantize(T["e_grp", a][:].rearrange("p g b j -> p (g b j)"), 1024, "e_q%d" % a)
+
+        def fi(tok, a, q):
+            if ("f_grp", a) not in T:
+                T["f_grp", a] = sb.tile([P, NR, 4], BF16, name="f_grp%d" % a, tag="f_grp%d" % a, align_bytes=64)
+            c = FI_V_COLS[a]
+            cols = slice(0, c) if q == 0 else slice(c, NR)
+            src = T["f_raw", a][:, :, cols].rearrange("p j r -> p r j")
+            if q == 0:
+                nc.vector.tensor_copy(out=T["f_grp", a][:, cols, :], in_=src)
+            else:
+                nc.scalar.copy(out=T["f_grp", a][:, cols, :], in_=src)
+
+        def qf(tok, a):
+            T["f_q", a] = quantize(T["f_grp", a][:].rearrange("p r j -> p (r j)"), 2048, "f_q%d" % a)
+
+        def s1(tok, a, g):
+            T["e_bank", a, g] = stage1(T["e_q", a], g, 1, "e_bank")
+
+        def ad(tok, a, g):
+            if g == 0:
+                T["a_grp", a] = sb.tile([P, 2, P, 4], BF16, name="a_grp", tag="a_grp", bufs=3, align_bytes=64)
+            nc.vector.tensor_tensor(
+                out=T["a_grp", a][:, g, :, :],
+                in0=T["e_bank", a, g][:].rearrange("p t b -> p b t"),
+                in1=T["nodeb", g][:],
+                op=ADD,
+            )
+
+        def qa(tok, a):
+            T["a_q", a] = quantize(T["a_grp", a][:].rearrange("p g b j -> p (g b j)"), 1024, "a_q%d" % a)
+
+        def s2(tok, a, g):
+            T["o_bank", a, g] = ps.tile([P, NR], F32, name="o_bank", tag="s2", bufs=3)
+            mx(T["o_bank", a, g][:], T["a_q", a], slice(g * P, (g + 1) * P), T["f_q", a], slice(0, NR))
+
+        def oc(tok, a, g):
+            if g == 0:
+                T["o_st", a] = sb.tile([P, 2, NR], F32, name="o_st", tag="o_st", bufs=4)
+            copy_engine(tok)(out=T["o_st", a][:, g, :], in_=T["o_bank", a, g][:])
+
+        def st(tok, a, g=None):
+            if g is None:
+                nc.sync.dma_start(out=out_view[:, :, a, :], in_=T["o_st", a][:])
+            else:
+                nc.sync.dma_start(out=out_view[:, g, a, :], in_=T["o_st", a][:, g, :])
+
+        ops = {"LW": LW, "LI": LI, "LE": LE, "LF": LF, "wtr": wtr, "wcp": wcp, "wq": wq, "itr": itr, "icp": icp,
+               "iq": iq, "nd": nd, "nb": nb, "tr": tr, "cp": cp, "qe": qe, "fi": fi, "qf": qf, "s1": s1, "ad": ad,
+               "qa": qa, "s2": s2, "oc": oc, "st": st}
+        for tok in ORDER.split(" "):
+            parts = tok.split("_")
+            ops[parts[0]](tok, *[int(x) for x in parts[1:]])

@@ -15,9 +15,9 @@ FLOPS = 2 * (NB + NB * NA) * NE * NP + 2 * NB * NA * NP * NR
 P = 128
 BANK_DT = F32
 ON_VECTOR = ['oc_7_1']
-FI_V_COLS = [224,224,224,224,224,224,224,224]
+FI_V_COLS = [288,288,288,288,192,192,0,0]
 SPLIT_STORES = [7]
-ORDER = """LF_0 LW_0 LW_1 LW_2 LW_3 LI LE_0 LF_1 LF_2 LE_1 LF_3 LF_4 LE_2 LF_5 LF_6 LE_3 LF_7 fi_0_0 fi_0_1 wtr_0 wcp_0 wtr_1 wcp_1 wtr_2 wcp_2 wtr_3 wcp_3 qf_0 wq_0 wq_1 itr icp wq_2 wq_3 tr_0 cp_0 iq tr_1 cp_1 nd_0 nd_1 fi_1_0 fi_1_1 nb_0 nb_1 qe_0 s1_0_0 s1_0_1 tr_2 cp_2 ad_0_0 ad_0_1 qe_1 s1_1_0 s1_1_1 tr_3 cp_3 qa_0 fi_2_0 fi_2_1 qf_1 s2_0_0 s2_0_1 oc_0_0 oc_0_1 st_0 ad_1_0 ad_1_1 qe_2 s1_2_0 s1_2_1 tr_4 cp_4 qa_1 fi_3_0 fi_3_1 qf_2 s2_1_0 s2_1_1 oc_1_0 oc_1_1 st_1 ad_2_0 ad_2_1 qe_3 s1_3_0 s1_3_1 tr_5 cp_5 qa_2 fi_4_0 fi_4_1 qf_3 s2_2_0 s2_2_1 oc_2_0 oc_2_1 st_2 ad_3_0 ad_3_1 qe_4 s1_4_0 s1_4_1 tr_6 cp_6 qa_3 fi_5_0 fi_5_1 qf_4 s2_3_0 s2_3_1 oc_3_0 oc_3_1 st_3 ad_4_0 ad_4_1 qe_5 s1_5_0 s1_5_1 tr_7 cp_7 qa_4 fi_6_0 fi_6_1 qf_5 s2_4_0 s2_4_1 oc_4_0 oc_4_1 st_4 ad_5_0 ad_5_1 qe_6 s1_6_0 s1_6_1 qa_5 fi_7_0 fi_7_1 qf_6 s2_5_0 s2_5_1 oc_5_0 oc_5_1 st_5 ad_6_0 ad_6_1 qe_7 s1_7_0 s1_7_1 qa_6 qf_7 s2_6_0 s2_6_1 oc_6_0 oc_6_1 st_6 ad_7_0 ad_7_1 qa_7 s2_7_0 s2_7_1 oc_7_0 st_7_0 oc_7_1 st_7_1"""
+ORDER = """LW_0 LF_0 LW_1 LW_2 LF_1 LW_3 LI LF_2 LE_0 LF_3 LE_1 LF_4 LF_5 LE_2 LF_6 LF_7 LE_3 wtr_0 fi_0_1 fi_0_0 wcp_0 wtr_1 wcp_1 wq_0 qf_0 fi_1_1 fi_1_0 wtr_2 wcp_2 wq_1 wtr_3 wcp_3 qf_1 wq_2 fi_2_1 fi_2_0 itr icp wq_3 qf_2 fi_3_1 fi_3_0 iq tr_0 cp_0 tr_1 cp_1 qf_3 nd_0 nd_1 nb_0 nb_1 fi_4_1 tr_2 cp_2 tr_3 cp_3 fi_5_1 qe_0 s1_0_0 s1_0_1 s1_1_0 tr_4 tr_5 ad_0_0 ad_0_1 s1_1_1 ad_1_0 qa_0 s2_0_0 s2_0_1 oc_0_0 oc_0_1 st_0 cp_4 ad_1_1 fi_4_0 qa_1 s2_1_0 s2_1_1 oc_1_0 oc_1_1 st_1 cp_5 fi_6_1 qe_1 s1_2_0 s1_2_1 s1_3_0 fi_5_0 tr_6 tr_7 ad_2_0 ad_2_1 s1_3_1 ad_3_0 qa_2 s2_2_0 s2_2_1 oc_2_0 oc_2_1 st_2 cp_6 ad_3_1 qf_4 qa_3 s2_3_0 s2_3_1 oc_3_0 oc_3_1 st_3 cp_7 qe_2 s1_4_0 s1_4_1 s1_5_0 qf_5 ad_4_0 ad_4_1 s1_5_1 ad_5_0 qa_4 s2_4_0 s2_4_1 oc_4_0 oc_4_1 st_4 fi_7_1 ad_5_1 qf_6 qa_5 s2_5_0 s2_5_1 oc_5_0 oc_5_1 st_5 qe_3 s1_6_0 s1_6_1 s1_7_0 ad_6_0 ad_6_1 s1_7_1 ad_7_0 qa_6 s2_6_0 s2_6_1 oc_6_0 oc_6_1 st_6 ad_7_1 qf_7 qa_7 s2_7_0 s2_7_1 oc_7_0 st_7_0 oc_7_1 st_7_1"""
 
 
 def tile_attributegnn_pa_kernel(tc, image_features, edge_attributes, linear_w, linear_b, fwd_proj, out):
@@ -127,10 +127,15 @@ def tile_attributegnn_pa_kernel(tc, image_features, edge_attributes, linear_w, l
             T["e_tp", a] = transposes([er[:, 0, a % 2, :], er[:, 1, a % 2, :]], "e_tp")
 
         def cp(tok, a):
-            T["e_grp", a] = copy_out(tok, T["e_tp", a], "e_grp", "e_grp", 4)
+            if a % 2 == 0:
+                T["e_grp", a // 2] = sb.tile([P, 2, 2, P, 4], BF16, name="e_grp", tag="e_grp", bufs=2, align_bytes=64)
+            copy_engine(tok)(
+                out=T["e_grp", a // 2][:, a % 2, :, :, :].bitcast(F32),
+                in_=T["e_tp", a][:].rearrange("p g u b -> p g b u"),
+            )
 
-        def qe(tok, a):
-            T["e_q", a] = quantize(T["e_grp", a][:].rearrange("p g b j -> p (g b j)"), 1024, "e_q%d" % a)
+        def qe(tok, i):
+            T["e_q", i] = quantize(T["e_grp", i][:].rearrange("p a g b j -> p (a g b j)"), 2048, "e_q%d" % i)
 
         def fi(tok, a, q):
             if ("f_grp", a) not in T:
@@ -147,7 +152,7 @@ def tile_attributegnn_pa_kernel(tc, image_features, edge_attributes, linear_w, l
             T["f_q", a] = quantize(T["f_grp", a][:].rearrange("p r j -> p (r j)"), 2048, "f_q%d" % a)
 
         def s1(tok, a, g):
-            T["e_bank", a, g] = stage1(T["e_q", a], g, 1, "e_bank")
+            T["e_bank", a, g] = stage1(T["e_q", a // 2], 2 * (a % 2) + g, 1, "e_bank")
 
         def ad(tok, a, g):
             if g == 0:

@@ -13,11 +13,13 @@ ADD = mybir.AluOpType.add
 NB, NA, NE, NP, NR = 256, 8, 512, 512, 512
 FLOPS = 2 * (NB + NB * NA) * NE * NP + 2 * NB * NA * NP * NR
 P = 128
-BANK_DT = F32
-ON_VECTOR = ['oc_7_1']
-FI_V_COLS = [288,288,288,288,192,192,0,0]
-SPLIT_STORES = [7]
-ORDER = """LW_0 LF_0 LW_1 LW_2 LF_1 LW_3 LI LF_2 LE_0 LF_3 LE_1 LF_4 LF_5 LE_2 LF_6 LF_7 LE_3 wtr_0 fi_0_1 fi_0_0 wcp_0 wtr_1 wcp_1 wq_0 qf_0 fi_1_1 fi_1_0 wtr_2 wcp_2 wq_1 wtr_3 wcp_3 qf_1 wq_2 fi_2_1 fi_2_0 itr icp wq_3 qf_2 fi_3_1 fi_3_0 iq tr_0 cp_0 tr_1 cp_1 qf_3 nd_0 nd_1 nb_0 nb_1 fi_4_1 tr_2 cp_2 tr_3 cp_3 fi_5_1 qe_0 s1_0_0 s1_0_1 s1_1_0 tr_4 tr_5 ad_0_0 ad_0_1 s1_1_1 ad_1_0 qa_0 s2_0_0 s2_0_1 oc_0_0 oc_0_1 st_0 cp_4 ad_1_1 fi_4_0 qa_1 s2_1_0 s2_1_1 oc_1_0 oc_1_1 st_1 cp_5 fi_6_1 qe_1 s1_2_0 s1_2_1 s1_3_0 fi_5_0 tr_6 tr_7 ad_2_0 ad_2_1 s1_3_1 ad_3_0 qa_2 s2_2_0 s2_2_1 oc_2_0 oc_2_1 st_2 cp_6 ad_3_1 qf_4 qa_3 s2_3_0 s2_3_1 oc_3_0 oc_3_1 st_3 cp_7 qe_2 s1_4_0 s1_4_1 s1_5_0 qf_5 ad_4_0 ad_4_1 s1_5_1 ad_5_0 qa_4 s2_4_0 s2_4_1 oc_4_0 oc_4_1 st_4 fi_7_1 ad_5_1 qf_6 qa_5 s2_5_0 s2_5_1 oc_5_0 oc_5_1 st_5 qe_3 s1_6_0 s1_6_1 s1_7_0 ad_6_0 ad_6_1 s1_7_1 ad_7_0 qa_6 s2_6_0 s2_6_1 oc_6_0 oc_6_1 st_6 ad_7_1 qf_7 qa_7 s2_7_0 s2_7_1 oc_7_0 st_7_0 oc_7_1 st_7_1"""
+PACK = 4
+STAGE1_PSUM = F32
+
+VECTOR_COLUMNS = (288, 288, 288, 288, 192, 192, 0, 0)
+
+VECTOR_FILL = (None, ("interleave", 4), ("interleave", 5), ("quantize", 4), ("quantize", 5), ("quantize", 6), None, ("quantize", 7))
+SCALAR_FILL = (None, 6, None, None, 7, None, None, None)
 
 
 def tile_attributegnn_pa_kernel(tc, image_features, edge_attributes, linear_w, linear_b, fwd_proj, out):
@@ -29,162 +31,271 @@ def tile_attributegnn_pa_kernel(tc, image_features, edge_attributes, linear_w, l
 
         ident = sb.tile([P, P], F32, name="ident", tag="ident")
         make_identity(nc, ident[:])
-        bias_sb = sb.tile([P, 4], BF16, name="bias_sb", tag="bias_sb")
-        nc.scalar.dma_start(out=bias_sb[:], in_=linear_b.rearrange("(p t) -> p t", t=4))
+        bias_sb = sb.tile([P, PACK], BF16, name="bias_sb", tag="bias_sb")
+        nc.scalar.dma_start(out=bias_sb[:], in_=linear_b.rearrange("(p t) -> p t", t=PACK))
 
-        w_view = linear_w.rearrange("(m t) k -> m t k", t=4)
+        w_view = linear_w.rearrange("(m t) k -> m t k", t=PACK)
         edge_view = edge_attributes.rearrange("(g p) a k -> p g a k", p=P)
         out_view = out.rearrange("(g p) a r -> p g a r", p=P)
-        T = {}
 
-        def copy_engine(tok):
-            return nc.vector.tensor_copy if tok in ON_VECTOR else nc.scalar.copy
+        w_raw, w_bank, w_grouped, w_mx = {}, {}, {}, {}
+        i_tiles = {}
+        e_raw, e_bank, e_grouped, e_mx = {}, {}, {}, {}
+        f_raw, f_grouped, f_mx = {}, {}, {}
+        node_psum, node_bias = {}, {}
+        edge_psum, agg_grouped, agg_mx = {}, {}, {}
+        out_psum, out_sb = {}, {}
 
-        def LW(tok, t):
-            T["w_raw", t] = sb.tile([P, 2 * NE], BF16, name="w_raw%d" % t, tag="w_raw%d" % t)
-            nc.sync.dma_start(out=T["w_raw", t][:], in_=w_view[:, t, :])
 
-        def LI(tok):
-            T["i_raw"] = sb.tile([P, 2, NE], BF16, name="i_raw", tag="i_raw")
-            nc.sync.dma_start(out=T["i_raw"][:], in_=image_features.rearrange("(g p) k -> p g k", p=P))
+        def load_weights(t):
+            w_raw[t] = sb.tile([P, 2 * NE], BF16, name="w_raw%d" % t, tag="w_raw%d" % t)
+            nc.sync.dma_start(out=w_raw[t][:], in_=w_view[:, t, :])
 
-        def LE(tok, i):
-            T["e_raw", i] = sb.tile([P, 2, 2, NE], BF16, name="e_raw%d" % i, tag="e_raw%d" % i)
-            nc.sync.dma_start(out=T["e_raw", i][:], in_=edge_view[:, :, 2 * i : 2 * i + 2, :])
+        def load_image():
+            i_tiles["raw"] = sb.tile([P, 2, NE], BF16, name="i_raw", tag="i_raw")
+            nc.sync.dma_start(out=i_tiles["raw"][:], in_=image_features.rearrange("(g p) k -> p g k", p=P))
 
-        def LF(tok, a):
-            T["f_raw", a] = sb.tile([P, 4, NR], BF16, name="f_raw%d" % a, tag="f_raw%d" % a)
-            nc.sync.dma_start(out=T["f_raw", a][:], in_=fwd_proj[a].rearrange("(p j) r -> p j r", j=4))
+        def load_edges(i):
+            e_raw[i] = sb.tile([P, 2, 2, NE], BF16, name="e_raw%d" % i, tag="e_raw%d" % i)
+            nc.sync.dma_start(out=e_raw[i][:], in_=edge_view[:, :, 2 * i : 2 * i + 2, :])
 
-        def transposes(srcs, name):
-            tp = ps.tile([P, 2, 2, P], F32, name=name, tag="tp", bufs=2)
+        def load_proj(a):
+            f_raw[a] = sb.tile([P, PACK, NR], BF16, name="f_raw%d" % a, tag="f_raw%d" % a)
+            nc.sync.dma_start(out=f_raw[a][:], in_=fwd_proj[a].rearrange("(p j) r -> p j r", j=PACK))
+
+
+        def transpose_two(sources, name):
+            bank = ps.tile([P, 2, 2, P], F32, name=name, tag="tp", bufs=2)
             for g in (0, 1):
-                words = srcs[g].bitcast(F32)
+                words = sources[g].bitcast(F32)
                 for u in (0, 1):
-                    nc.tensor.transpose(tp[:, g, u, :], words[:, u : NE // 2 : 2], ident[:])
-            return tp
+                    nc.tensor.transpose(bank[:, g, u, :], words[:, u : NE // 2 : 2], ident[:])
+            return bank
 
-        def copy_out(tok, tp, name, tag, bufs):
-            grp = sb.tile([P, 2, P, 4], BF16, name=name, tag=tag, bufs=bufs, align_bytes=64)
-            copy_engine(tok)(out=grp[:].bitcast(F32), in_=tp[:].rearrange("p g u b -> p g b u"))
-            return grp
+        def copy_grouped(bank, name, tag, bufs):
+            grouped = sb.tile([P, 2, P, PACK], BF16, name=name, tag=tag, bufs=bufs, align_bytes=64)
+            nc.scalar.copy(out=grouped[:].bitcast(F32), in_=bank[:].rearrange("p g u b -> p g b u"))
+            return grouped
 
-        def quantize(grp_flat, width, name):
-            codes = sb.tile([P, width // 4], U32, name=name + "_c", tag=name + "_c", align_bytes=64)
-            scales = sb.tile([P, width // 4], U8, name=name + "_s", tag=name + "_s", align_bytes=64)
-            nc.vector.quantize_mx(out=codes[:].bitcast(FP8X4), scales=scales[:], in_=grp_flat)
+        def quantize(grouped_flat, width, name):
+            codes = sb.tile([P, width // PACK], U32, name=name + "_c", tag=name + "_c", align_bytes=64)
+            scales = sb.tile([P, width // PACK], U8, name=name + "_s", tag=name + "_s", align_bytes=64)
+            nc.vector.quantize_mx(out=codes[:].bitcast(FP8X4), scales=scales[:], in_=grouped_flat)
             return codes, scales
 
-        def mx(out_ap, lhs, lcols, rhs, rcols):
+        def one_pass(out_ap, stationary, s_cols, moving, m_cols):
             nc.tensor.matmul_mx(
                 out=out_ap,
-                lhsT=lhs[0][:, lcols].bitcast(FP8X4),
-                lhsT_scale=lhs[1][:, lcols],
-                rhs=rhs[0][:, rcols].bitcast(FP8X4),
-                rhs_scale=rhs[1][:, rcols],
+                lhsT=stationary[0][:, s_cols].bitcast(FP8X4),
+                lhsT_scale=stationary[1][:, s_cols],
+                rhs=moving[0][:, m_cols].bitcast(FP8X4),
+                rhs_scale=moving[1][:, m_cols],
                 start=True,
                 stop=True,
             )
 
-        def stage1(x_q, g, h, name):
-            bank = ps.tile([P, 4, P], BANK_DT, name=name, tag="s1", bufs=3)
-            for t in range(4):
-                mx(bank[:, t, :], T["w_q", t], slice(h * P, (h + 1) * P), x_q, slice(g * P, (g + 1) * P))
-            return bank
+        def stage1(x_mx, g, half, name):
+            tile = ps.tile([P, PACK, P], STAGE1_PSUM, name=name, tag="s1", bufs=3)
+            for t in range(PACK):
+                one_pass(tile[:, t, :], w_mx[t], slice(half * P, (half + 1) * P), x_mx, slice(g * P, (g + 1) * P))
+            return tile
 
-        def wtr(tok, t):
-            T["w_tp", t] = transposes([T["w_raw", t][:, 0:NE], T["w_raw", t][:, NE : 2 * NE]], "w_tp")
 
-        def wcp(tok, t):
-            T["w_grp", t] = copy_out(tok, T["w_tp", t], "w_grp%d" % t, "w_grp%d" % t, 1)
+        def transpose_weights(t):
+            w_bank[t] = transpose_two([w_raw[t][:, 0:NE], w_raw[t][:, NE : 2 * NE]], "w_tp")
 
-        def wq(tok, t):
-            T["w_q", t] = quantize(T["w_grp", t][:].rearrange("p g b j -> p (g b j)"), 1024, "w_q%d" % t)
+        def copy_weights(t):
+            w_grouped[t] = copy_grouped(w_bank[t], "w_grp%d" % t, "w_grp%d" % t, 1)
 
-        def itr(tok):
-            T["i_tp"] = transposes([T["i_raw"][:, 0, :], T["i_raw"][:, 1, :]], "i_tp")
+        def quantize_weights(t):
+            w_mx[t] = quantize(w_grouped[t][:].rearrange("p g b j -> p (g b j)"), 2 * P * PACK, "w_q%d" % t)
 
-        def icp(tok):
-            T["i_grp"] = copy_out(tok, T["i_tp"], "i_grp", "i_grp", 1)
+        def transpose_image():
+            i_tiles["bank"] = transpose_two([i_tiles["raw"][:, 0, :], i_tiles["raw"][:, 1, :]], "i_tp")
 
-        def iq(tok):
-            T["i_q"] = quantize(T["i_grp"][:].rearrange("p g b j -> p (g b j)"), 1024, "i_q")
+        def copy_image():
+            i_tiles["grouped"] = copy_grouped(i_tiles["bank"], "i_grp", "i_grp", 1)
 
-        def nd(tok, g):
-            T["n_bank", g] = stage1(T["i_q"], g, 0, "n_bank")
+        def quantize_image():
+            i_tiles["mx"] = quantize(i_tiles["grouped"][:].rearrange("p g b j -> p (g b j)"), 2 * P * PACK, "i_q")
 
-        def nb(tok, g):
-            T["nodeb", g] = sb.tile([P, P, 4], F32, name="nodeb%d" % g, tag="nodeb%d" % g)
+        def node_passes(g):
+            node_psum[g] = stage1(i_tiles["mx"], g, 0, "n_bank")
+
+        def node_plus_bias(g):
+            node_bias[g] = sb.tile([P, P, PACK], F32, name="nodeb%d" % g, tag="nodeb%d" % g)
             nc.vector.tensor_tensor(
-                out=T["nodeb", g][:],
-                in0=T["n_bank", g][:].rearrange("p t b -> p b t"),
-                in1=bias_sb[:].unsqueeze(1).to_broadcast([P, P, 4]),
+                out=node_bias[g][:],
+                in0=node_psum[g][:].rearrange("p t b -> p b t"),
+                in1=bias_sb[:].unsqueeze(1).to_broadcast([P, P, PACK]),
                 op=ADD,
             )
 
-        def tr(tok, a):
-            er = T["e_raw", a // 2]
-            T["e_tp", a] = transposes([er[:, 0, a % 2, :], er[:, 1, a % 2, :]], "e_tp")
 
-        def cp(tok, a):
-            if a % 2 == 0:
-                T["e_grp", a // 2] = sb.tile([P, 2, 2, P, 4], BF16, name="e_grp", tag="e_grp", bufs=2, align_bytes=64)
-            copy_engine(tok)(
-                out=T["e_grp", a // 2][:, a % 2, :, :, :].bitcast(F32),
-                in_=T["e_tp", a][:].rearrange("p g u b -> p g b u"),
-            )
+        def transpose_edges(a):
+            raw = e_raw[a // 2]
+            e_bank[a] = transpose_two([raw[:, 0, a % 2, :], raw[:, 1, a % 2, :]], "e_tp")
 
-        def qe(tok, i):
-            T["e_q", i] = quantize(T["e_grp", i][:].rearrange("p a g b j -> p (a g b j)"), 2048, "e_q%d" % i)
+        def copy_edges(a):
+            e_grouped[a] = copy_grouped(e_bank[a], "e_grp", "e_grp", 4)
 
-        def fi(tok, a, q):
-            if ("f_grp", a) not in T:
-                T["f_grp", a] = sb.tile([P, NR, 4], BF16, name="f_grp%d" % a, tag="f_grp%d" % a, align_bytes=64)
-            c = FI_V_COLS[a]
-            cols = slice(0, c) if q == 0 else slice(c, NR)
-            src = T["f_raw", a][:, :, cols].rearrange("p j r -> p r j")
-            if q == 0:
-                nc.vector.tensor_copy(out=T["f_grp", a][:, cols, :], in_=src)
-            else:
-                nc.scalar.copy(out=T["f_grp", a][:, cols, :], in_=src)
+        def quantize_edges(a):
+            e_mx[a] = quantize(e_grouped[a][:].rearrange("p g b j -> p (g b j)"), 2 * P * PACK, "e_q%d" % a)
 
-        def qf(tok, a):
-            T["f_q", a] = quantize(T["f_grp", a][:].rearrange("p r j -> p (r j)"), 2048, "f_q%d" % a)
+        def edge_passes(a, g):
+            edge_psum[a, g] = stage1(e_mx[a], g, 1, "e_bank")
 
-        def s1(tok, a, g):
-            T["e_bank", a, g] = stage1(T["e_q", a // 2], 2 * (a % 2) + g, 1, "e_bank")
-
-        def ad(tok, a, g):
+        def add_node(a, g):
             if g == 0:
-                T["a_grp", a] = sb.tile([P, 2, P, 4], BF16, name="a_grp", tag="a_grp", bufs=3, align_bytes=64)
+                agg_grouped[a] = sb.tile([P, 2, P, PACK], BF16, name="a_grp", tag="a_grp", bufs=3, align_bytes=64)
             nc.vector.tensor_tensor(
-                out=T["a_grp", a][:, g, :, :],
-                in0=T["e_bank", a, g][:].rearrange("p t b -> p b t"),
-                in1=T["nodeb", g][:],
+                out=agg_grouped[a][:, g, :, :],
+                in0=edge_psum[a, g][:].rearrange("p t b -> p b t"),
+                in1=node_bias[g][:],
                 op=ADD,
             )
 
-        def qa(tok, a):
-            T["a_q", a] = quantize(T["a_grp", a][:].rearrange("p g b j -> p (g b j)"), 1024, "a_q%d" % a)
+        def quantize_agg(a):
+            agg_mx[a] = quantize(agg_grouped[a][:].rearrange("p g b j -> p (g b j)"), 2 * P * PACK, "a_q%d" % a)
 
-        def s2(tok, a, g):
-            T["o_bank", a, g] = ps.tile([P, NR], F32, name="o_bank", tag="s2", bufs=3)
-            mx(T["o_bank", a, g][:], T["a_q", a], slice(g * P, (g + 1) * P), T["f_q", a], slice(0, NR))
 
-        def oc(tok, a, g):
-            if g == 0:
-                T["o_st", a] = sb.tile([P, 2, NR], F32, name="o_st", tag="o_st", bufs=4)
-            copy_engine(tok)(out=T["o_st", a][:, g, :], in_=T["o_bank", a, g][:])
+        def interleave_proj(a, engine_copy, cols):
+            if a not in f_grouped:
+                f_grouped[a] = sb.tile([P, NR, PACK], BF16, name="f_grp%d" % a, tag="f_grp%d" % a, align_bytes=64)
+            engine_copy(out=f_grouped[a][:, cols, :], in_=f_raw[a][:, :, cols].rearrange("p j r -> p r j"))
 
-        def st(tok, a, g=None):
-            if g is None:
-                nc.sync.dma_start(out=out_view[:, :, a, :], in_=T["o_st", a][:])
+        def interleave_proj_vector(a):
+            interleave_proj(a, nc.vector.tensor_copy, slice(0, VECTOR_COLUMNS[a]))
+
+        def interleave_proj_scalar(a):
+            interleave_proj(a, nc.scalar.copy, slice(VECTOR_COLUMNS[a], NR))
+
+        def quantize_proj(a):
+            f_mx[a] = quantize(f_grouped[a][:].rearrange("p r j -> p (r j)"), NR * PACK, "f_q%d" % a)
+
+
+        def out_passes(a):
+            for g in (0, 1):
+                out_psum[a, g] = ps.tile([P, NR], F32, name="o_bank", tag="s2", bufs=3)
+                one_pass(out_psum[a, g][:], agg_mx[a], slice(g * P, (g + 1) * P), f_mx[a], slice(0, NR))
+
+        def copy_and_store(a):
+            out_sb[a] = sb.tile([P, 2, NR], F32, name="o_st", tag="o_st", bufs=4)
+            if a < NA - 1:
+                for g in (0, 1):
+                    nc.scalar.copy(out=out_sb[a][:, g, :], in_=out_psum[a, g][:])
+                nc.sync.dma_start(out=out_view[:, :, a, :], in_=out_sb[a][:])
             else:
-                nc.sync.dma_start(out=out_view[:, g, a, :], in_=T["o_st", a][:, g, :])
+                nc.scalar.copy(out=out_sb[a][:, 0, :], in_=out_psum[a, 0][:])
+                nc.sync.dma_start(out=out_view[:, 0, a, :], in_=out_sb[a][:, 0, :])
+                nc.vector.tensor_copy(out=out_sb[a][:, 1, :], in_=out_psum[a, 1][:])
+                nc.sync.dma_start(out=out_view[:, 1, a, :], in_=out_sb[a][:, 1, :])
 
-        ops = {"LW": LW, "LI": LI, "LE": LE, "LF": LF, "wtr": wtr, "wcp": wcp, "wq": wq, "itr": itr, "icp": icp,
-               "iq": iq, "nd": nd, "nb": nb, "tr": tr, "cp": cp, "qe": qe, "fi": fi, "qf": qf, "s1": s1, "ad": ad,
-               "qa": qa, "s2": s2, "oc": oc, "st": st}
-        for tok in ORDER.split(" "):
-            parts = tok.split("_")
-            ops[parts[0]](tok, *[int(x) for x in parts[1:]])
+        def vector_fill(slot):
+            if VECTOR_FILL[slot] is not None:
+                what, a = VECTOR_FILL[slot]
+                if what == "interleave":
+                    interleave_proj_vector(a)
+                else:
+                    quantize_proj(a)
+
+        def scalar_fill(slot):
+            if SCALAR_FILL[slot] is not None:
+                interleave_proj_scalar(SCALAR_FILL[slot])
+
+        load_weights(0)
+        load_proj(0)
+        load_weights(1)
+        load_weights(2)
+        load_proj(1)
+        load_weights(3)
+        load_image()
+        load_proj(2)
+        load_edges(0)
+        load_proj(3)
+        load_edges(1)
+        load_proj(4)
+        load_proj(5)
+        load_edges(2)
+        load_proj(6)
+        load_proj(7)
+        load_edges(3)
+
+        transpose_weights(0)
+        interleave_proj_scalar(0)
+        interleave_proj_vector(0)
+        copy_weights(0)
+        transpose_weights(1)
+        copy_weights(1)
+        quantize_weights(0)
+        quantize_proj(0)
+        interleave_proj_scalar(1)
+        interleave_proj_vector(1)
+        transpose_weights(2)
+        copy_weights(2)
+        quantize_weights(1)
+        transpose_weights(3)
+        copy_weights(3)
+        quantize_proj(1)
+        quantize_weights(2)
+        interleave_proj_scalar(2)
+        interleave_proj_vector(2)
+        transpose_image()
+        copy_image()
+        quantize_weights(3)
+        quantize_proj(2)
+        interleave_proj_scalar(3)
+        interleave_proj_vector(3)
+        quantize_image()
+        transpose_edges(0)
+        copy_edges(0)
+        transpose_edges(1)
+        copy_edges(1)
+        quantize_proj(3)
+
+        node_passes(0)
+        node_passes(1)
+        quantize_edges(0)
+        quantize_edges(1)
+        node_plus_bias(0)
+        edge_passes(0, 0)
+        node_plus_bias(1)
+        edge_passes(0, 1)
+        edge_passes(1, 0)
+        interleave_proj_scalar(4)
+        interleave_proj_scalar(5)
+        transpose_edges(2)
+        copy_edges(2)
+        transpose_edges(3)
+        copy_edges(3)
+
+        for j in range(NA // 2):
+            first, second = 2 * j, 2 * j + 1
+            vector_fill(2 * j)
+            add_node(first, 0)
+            add_node(first, 1)
+            edge_passes(second, 1)
+            add_node(second, 0)
+            quantize_agg(first)
+            out_passes(first)
+            if first + 4 < NA:
+                transpose_edges(first + 4)
+                transpose_edges(second + 4)
+            copy_and_store(first)
+            if first + 4 < NA:
+                copy_edges(first + 4)
+            scalar_fill(2 * j)
+            add_node(second, 1)
+            vector_fill(2 * j + 1)
+            quantize_agg(second)
+            out_passes(second)
+            copy_and_store(second)
+            if first + 4 < NA:
+                copy_edges(second + 4)
+            scalar_fill(2 * j + 1)
+            if first + 2 < NA:
+                quantize_edges(first + 2)
+                quantize_edges(second + 2)
+                edge_passes(first + 2, 0)
+                edge_passes(first + 2, 1)
+                edge_passes(second + 2, 0)

from contextlib import ExitStack

import concourse.mybir as mybir
from concourse.masks import make_identity

F32 = mybir.dt.float32
BF16 = mybir.dt.bfloat16
U32 = mybir.dt.uint32
U8 = mybir.dt.uint8
FP8X4 = mybir.dt.float8_e4m3fn_x4
ADD = mybir.AluOpType.add

NB, NA, NE, NP, NR = 256, 8, 512, 512, 512
FLOPS = 2 * (NB + NB * NA) * NE * NP + 2 * NB * NA * NP * NR
P = 128
PACK = 4
STAGE1_PSUM = F32

VECTOR_COLUMNS = (288, 288, 288, 288, 192, 192, 0, 0)

VECTOR_FILL = (None, ("interleave", 4), ("interleave", 5), ("quantize", 4), ("quantize", 5), ("quantize", 6), None, ("quantize", 7))
SCALAR_FILL = (None, 6, None, None, 7, None, None, None)


def tile_attributegnn_pa_kernel(tc, image_features, edge_attributes, linear_w, linear_b, fwd_proj, out):
    nc = tc.nc
    with ExitStack() as ctx:
        sb = ctx.enter_context(tc.tile_pool(name="sb", bufs=1))
        ps = ctx.enter_context(tc.psum_pool(name="ps", bufs=1))
        ctx.enter_context(tc.manual_schedule())

        ident = sb.tile([P, P], F32, name="ident", tag="ident")
        make_identity(nc, ident[:])
        bias_sb = sb.tile([P, PACK], BF16, name="bias_sb", tag="bias_sb")
        nc.scalar.dma_start(out=bias_sb[:], in_=linear_b.rearrange("(p t) -> p t", t=PACK))

        w_view = linear_w.rearrange("(m t) k -> m t k", t=PACK)
        edge_view = edge_attributes.rearrange("(g p) a k -> p g a k", p=P)
        out_view = out.rearrange("(g p) a r -> p g a r", p=P)

        w_raw, w_bank, w_grouped, w_mx = {}, {}, {}, {}
        i_tiles = {}
        e_raw, e_bank, e_grouped, e_mx = {}, {}, {}, {}
        f_raw, f_grouped, f_mx = {}, {}, {}
        node_psum, node_bias = {}, {}
        edge_psum, agg_grouped, agg_mx = {}, {}, {}
        out_psum, out_sb = {}, {}


        def load_weights(t):
            w_raw[t] = sb.tile([P, 2 * NE], BF16, name="w_raw%d" % t, tag="w_raw%d" % t)
            nc.sync.dma_start(out=w_raw[t][:], in_=w_view[:, t, :])

        def load_image():
            i_tiles["raw"] = sb.tile([P, 2, NE], BF16, name="i_raw", tag="i_raw")
            nc.sync.dma_start(out=i_tiles["raw"][:], in_=image_features.rearrange("(g p) k -> p g k", p=P))

        def load_edges(i):
            e_raw[i] = sb.tile([P, 2, 2, NE], BF16, name="e_raw%d" % i, tag="e_raw%d" % i)
            nc.sync.dma_start(out=e_raw[i][:], in_=edge_view[:, :, 2 * i : 2 * i + 2, :])

        def load_proj(a):
            f_raw[a] = sb.tile([P, PACK, NR], BF16, name="f_raw%d" % a, tag="f_raw%d" % a)
            nc.sync.dma_start(out=f_raw[a][:], in_=fwd_proj[a].rearrange("(p j) r -> p j r", j=PACK))


        def transpose_two(sources, name):
            bank = ps.tile([P, 2, 2, P], F32, name=name, tag="tp", bufs=2)
            for g in (0, 1):
                words = sources[g].bitcast(F32)
                for u in (0, 1):
                    nc.tensor.transpose(bank[:, g, u, :], words[:, u : NE // 2 : 2], ident[:])
            return bank

        def copy_grouped(bank, name, tag, bufs):
            grouped = sb.tile([P, 2, P, PACK], BF16, name=name, tag=tag, bufs=bufs, align_bytes=64)
            nc.scalar.copy(out=grouped[:].bitcast(F32), in_=bank[:].rearrange("p g u b -> p g b u"))
            return grouped

        def quantize(grouped_flat, width, name):
            codes = sb.tile([P, width // PACK], U32, name=name + "_c", tag=name + "_c", align_bytes=64)
            scales = sb.tile([P, width // PACK], U8, name=name + "_s", tag=name + "_s", align_bytes=64)
            nc.vector.quantize_mx(out=codes[:].bitcast(FP8X4), scales=scales[:], in_=grouped_flat)
            return codes, scales

        def one_pass(out_ap, stationary, s_cols, moving, m_cols):
            nc.tensor.matmul_mx(
                out=out_ap,
                lhsT=stationary[0][:, s_cols].bitcast(FP8X4),
                lhsT_scale=stationary[1][:, s_cols],
                rhs=moving[0][:, m_cols].bitcast(FP8X4),
                rhs_scale=moving[1][:, m_cols],
                start=True,
                stop=True,
            )

        def stage1(x_mx, g, half, name):
            tile = ps.tile([P, PACK, P], STAGE1_PSUM, name=name, tag="s1", bufs=3)
            for t in range(PACK):
                one_pass(tile[:, t, :], w_mx[t], slice(half * P, (half + 1) * P), x_mx, slice(g * P, (g + 1) * P))
            return tile


        def transpose_weights(t):
            w_bank[t] = transpose_two([w_raw[t][:, 0:NE], w_raw[t][:, NE : 2 * NE]], "w_tp")

        def copy_weights(t):
            w_grouped[t] = copy_grouped(w_bank[t], "w_grp%d" % t, "w_grp%d" % t, 1)

        def quantize_weights(t):
            w_mx[t] = quantize(w_grouped[t][:].rearrange("p g b j -> p (g b j)"), 2 * P * PACK, "w_q%d" % t)

        def transpose_image():
            i_tiles["bank"] = transpose_two([i_tiles["raw"][:, 0, :], i_tiles["raw"][:, 1, :]], "i_tp")

        def copy_image():
            i_tiles["grouped"] = copy_grouped(i_tiles["bank"], "i_grp", "i_grp", 1)

        def quantize_image():
            i_tiles["mx"] = quantize(i_tiles["grouped"][:].rearrange("p g b j -> p (g b j)"), 2 * P * PACK, "i_q")

        def node_passes(g):
            node_psum[g] = stage1(i_tiles["mx"], g, 0, "n_bank")

        def node_plus_bias(g):
            node_bias[g] = sb.tile([P, P, PACK], F32, name="nodeb%d" % g, tag="nodeb%d" % g)
            nc.vector.tensor_tensor(
                out=node_bias[g][:],
                in0=node_psum[g][:].rearrange("p t b -> p b t"),
                in1=bias_sb[:].unsqueeze(1).to_broadcast([P, P, PACK]),
                op=ADD,
            )


        def transpose_edges(a):
            raw = e_raw[a // 2]
            e_bank[a] = transpose_two([raw[:, 0, a % 2, :], raw[:, 1, a % 2, :]], "e_tp")

        def copy_edges(a):
            e_grouped[a] = copy_grouped(e_bank[a], "e_grp", "e_grp", 4)

        def quantize_edges(a):
            e_mx[a] = quantize(e_grouped[a][:].rearrange("p g b j -> p (g b j)"), 2 * P * PACK, "e_q%d" % a)

        def edge_passes(a, g):
            edge_psum[a, g] = stage1(e_mx[a], g, 1, "e_bank")

        def add_node(a, g):
            if g == 0:
                agg_grouped[a] = sb.tile([P, 2, P, PACK], BF16, name="a_grp", tag="a_grp", bufs=3, align_bytes=64)
            nc.vector.tensor_tensor(
                out=agg_grouped[a][:, g, :, :],
                in0=edge_psum[a, g][:].rearrange("p t b -> p b t"),
                in1=node_bias[g][:],
                op=ADD,
            )

        def quantize_agg(a):
            agg_mx[a] = quantize(agg_grouped[a][:].rearrange("p g b j -> p (g b j)"), 2 * P * PACK, "a_q%d" % a)


        def interleave_proj(a, engine_copy, cols):
            if a not in f_grouped:
                f_grouped[a] = sb.tile([P, NR, PACK], BF16, name="f_grp%d" % a, tag="f_grp%d" % a, align_bytes=64)
            engine_copy(out=f_grouped[a][:, cols, :], in_=f_raw[a][:, :, cols].rearrange("p j r -> p r j"))

        def interleave_proj_vector(a):
            interleave_proj(a, nc.vector.tensor_copy, slice(0, VECTOR_COLUMNS[a]))

        def interleave_proj_scalar(a):
            interleave_proj(a, nc.scalar.copy, slice(VECTOR_COLUMNS[a], NR))

        def quantize_proj(a):
            f_mx[a] = quantize(f_grouped[a][:].rearrange("p r j -> p (r j)"), NR * PACK, "f_q%d" % a)


        def out_passes(a):
            for g in (0, 1):
                out_psum[a, g] = ps.tile([P, NR], F32, name="o_bank", tag="s2", bufs=3)
                one_pass(out_psum[a, g][:], agg_mx[a], slice(g * P, (g + 1) * P), f_mx[a], slice(0, NR))

        def copy_and_store(a):
            out_sb[a] = sb.tile([P, 2, NR], F32, name="o_st", tag="o_st", bufs=4)
            if a < NA - 1:
                for g in (0, 1):
                    nc.scalar.copy(out=out_sb[a][:, g, :], in_=out_psum[a, g][:])
                nc.sync.dma_start(out=out_view[:, :, a, :], in_=out_sb[a][:])
            else:
                nc.scalar.copy(out=out_sb[a][:, 0, :], in_=out_psum[a, 0][:])
                nc.sync.dma_start(out=out_view[:, 0, a, :], in_=out_sb[a][:, 0, :])
                nc.vector.tensor_copy(out=out_sb[a][:, 1, :], in_=out_psum[a, 1][:])
                nc.sync.dma_start(out=out_view[:, 1, a, :], in_=out_sb[a][:, 1, :])

        def vector_fill(slot):
            if VECTOR_FILL[slot] is not None:
                what, a = VECTOR_FILL[slot]
                if what == "interleave":
                    interleave_proj_vector(a)
                else:
                    quantize_proj(a)

        def scalar_fill(slot):
            if SCALAR_FILL[slot] is not None:
                interleave_proj_scalar(SCALAR_FILL[slot])

        load_weights(0)
        load_proj(0)
        load_weights(1)
        load_weights(2)
        load_proj(1)
        load_weights(3)
        load_image()
        load_proj(2)
        load_edges(0)
        load_proj(3)
        load_edges(1)
        load_proj(4)
        load_proj(5)
        load_edges(2)
        load_proj(6)
        load_proj(7)
        load_edges(3)

        transpose_weights(0)
        interleave_proj_scalar(0)
        interleave_proj_vector(0)
        copy_weights(0)
        transpose_weights(1)
        copy_weights(1)
        quantize_weights(0)
        quantize_proj(0)
        interleave_proj_scalar(1)
        interleave_proj_vector(1)
        transpose_weights(2)
        copy_weights(2)
        quantize_weights(1)
        transpose_weights(3)
        copy_weights(3)
        quantize_proj(1)
        quantize_weights(2)
        interleave_proj_scalar(2)
        interleave_proj_vector(2)
        transpose_image()
        copy_image()
        quantize_weights(3)
        quantize_proj(2)
        interleave_proj_scalar(3)
        interleave_proj_vector(3)
        quantize_image()
        transpose_edges(0)
        copy_edges(0)
        transpose_edges(1)
        copy_edges(1)
        quantize_proj(3)

        node_passes(0)
        node_passes(1)
        quantize_edges(0)
        quantize_edges(1)
        node_plus_bias(0)
        edge_passes(0, 0)
        node_plus_bias(1)
        edge_passes(0, 1)
        edge_passes(1, 0)
        interleave_proj_scalar(4)
        interleave_proj_scalar(5)
        transpose_edges(2)
        copy_edges(2)
        transpose_edges(3)
        copy_edges(3)

        for j in range(NA // 2):
            first, second = 2 * j, 2 * j + 1
            vector_fill(2 * j)
            add_node(first, 0)
            add_node(first, 1)
            edge_passes(second, 1)
            add_node(second, 0)
            quantize_agg(first)
            out_passes(first)
            if first + 4 < NA:
                transpose_edges(first + 4)
                transpose_edges(second + 4)
            copy_and_store(first)
            if first + 4 < NA:
                copy_edges(first + 4)
            scalar_fill(2 * j)
            add_node(second, 1)
            vector_fill(2 * j + 1)
            quantize_agg(second)
            out_passes(second)
            copy_and_store(second)
            if first + 4 < NA:
                copy_edges(second + 4)
            scalar_fill(2 * j + 1)
            if first + 2 < NA:
                quantize_edges(first + 2)
                quantize_edges(second + 2)
                edge_passes(first + 2, 0)
                edge_passes(first + 2, 1)
                edge_passes(second + 2, 0)
